import numpy as np
import ml_dtypes


def mxq(x, axis, fmt="e4m3"):
    dtype, down = {"e4m3": (ml_dtypes.float8_e4m3fn, 7), "e5m2": (ml_dtypes.float8_e5m2, 14)}[fmt]
    v = np.moveaxis(np.asarray(x, np.float32).astype(ml_dtypes.bfloat16).astype(np.float64), axis, -1)
    blocks = v.reshape(v.shape[:-1] + (-1, 32))
    amax = np.abs(blocks).max(-1, keepdims=True)
    byte = np.maximum(np.where(amax > 0, np.frexp(amax)[1] - 1 + 127, 0) - down, 1)
    scale = np.exp2(byte - 127.0)
    codes = (blocks / scale).astype(np.float32).astype(dtype).astype(np.float64)
    return np.moveaxis((codes * scale).reshape(v.shape), -1, axis)


WIDE = False


def mx_kscale(k):
    if not WIDE:
        return np.ones(k)
    levels = np.array([10, -10, 5, -5, 0])
    a = np.random.permutation(np.resize(levels, k // 512 * 4)).reshape(k // 512, 4)
    idx = np.arange(k)
    return np.exp2(a[idx // 512, idx % 128 // 32])


BF16 = ml_dtypes.bfloat16


def bf(x):
    return np.asarray(x, np.float32).astype(BF16)


def f64(x):
    return np.asarray(x).astype(np.float64)


B, DIM, D2, T = 8, 128, 512, 512


def setup_inputs():
    s, t = mx_kscale(D2), mx_kscale(T)
    es = 0.25 * s[None, :, None] * t[None, None, :]
    ss = 0.044 * np.sqrt(D2) / t[None, :, None]
    ps = 2.0 / np.sqrt(D2) / s[None, :]
    return {"E_re": bf(np.random.standard_normal((B, D2, T)) * es),
            "E_im": bf(np.random.standard_normal((B, D2, T)) * es),
            "S_re": bf(np.random.standard_normal((B, T, T)) * ss),
            "S_im": bf(np.random.standard_normal((B, T, T)) * ss),
            "WPV_re": bf(np.random.standard_normal((DIM, D2)) * ps),
            "WPV_im": bf(np.random.standard_normal((DIM, D2)) * ps)}


def reference(E_re, E_im, S_re, S_im, WPV_re, WPV_im):
    causal = np.triu(np.ones((T, T), dtype=bool))
    sr = mxq(np.where(causal, f64(S_re), 0.0), 1, "e4m3")
    si = mxq(np.where(causal, f64(S_im), 0.0), 1, "e4m3")
    er = mxq(f64(E_re), 2, "e4m3")
    ei = mxq(f64(E_im), 2, "e4m3")
    v_re = (er @ sr) - (ei @ si)
    v_im = (er @ si) + (ei @ sr)
    vr = mxq(v_re, 1, "e4m3")
    vi = mxq(v_im, 1, "e4m3")
    pr = mxq(f64(WPV_re), 1, "e4m3")
    pi = mxq(f64(WPV_im), 1, "e4m3")
    o_re = (pr @ vr) - (pi @ vi)
    o_im = (pr @ vi) + (pi @ vr)
    rho = np.maximum(np.arange(T, dtype=np.float64), 1.0)
    return o_re / rho[None, None, :], o_im / rho[None, None, :]

@@ -1,0 +1,256 @@
+from contextlib import ExitStack
+
+import concourse.mybir as mybir
+from concourse.masks import make_identity
+
+F32 = mybir.dt.float32
+BF16 = mybir.dt.bfloat16
+I32 = mybir.dt.int32
+U32 = mybir.dt.uint32
+U8 = mybir.dt.uint8
+FP8X4 = mybir.dt.float8_e4m3fn_x4
+ALU = mybir.AluOpType
+
+B = 8
+O = 128
+C = 512
+T = 512
+P = 128
+PACK = 4
+HALF = T // 2
+RE = 0
+IM = 1
+NEG_IM = 2
+
+RAW_BUFS = 4
+J_VECTOR = 320
+
+FLOPS = 4 * 2 * B * C * T * T + 4 * 2 * B * O * C * T
+
+
+def tile_autoregressivelsa_pb_t_kernel(
+    tc, E_re, E_im, S_re, S_im, WPV_re, WPV_im, out_re, out_im
+):
+    nc = tc.nc
+    E_parts = (E_re, E_im)
+    S_parts = (S_re, S_im)
+    W_parts = (WPV_re, WPV_im)
+    out_parts = (out_re, out_im)
+
+    with ExitStack() as ctx:
+        const = ctx.enter_context(tc.tile_pool(name="const", bufs=1))
+        e_pool = ctx.enter_context(tc.tile_pool(name="e_raw", bufs=RAW_BUFS))
+        work = ctx.enter_context(tc.tile_pool(name="work", bufs=2))
+        out_pool = ctx.enter_context(tc.tile_pool(name="out", bufs=3))
+        psum = ctx.enter_context(tc.psum_pool(name="psum", bufs=8))
+
+        e_raw = {}
+
+        def load_E(b):
+            e_raw[b] = e_pool.tile([P, 2, PACK, T], BF16, name="e_raw")
+            for part in (RE, IM):
+                nc.sync.dma_start(
+                    out=e_raw[b][:, part],
+                    in_=E_parts[part][b].rearrange("(p t) i -> p t i", t=PACK),
+                )
+
+        s_raw = [
+            const.tile([P, 2, PACK, T], BF16, name="s_raw%d" % k) for k in range(RAW_BUFS)
+        ]
+        for k in range(RAW_BUFS):
+            nc.vector.memset(s_raw[k][:, :, 2:4, 0:HALF], 0.0)
+
+        def load_S(b):
+            dst = s_raw[b % RAW_BUFS]
+            for part in (RE, IM):
+                nc.sync.dma_start(
+                    out=dst[:, part, 0:2, :],
+                    in_=S_parts[part][b, 0:HALF, :].rearrange("(p e) j -> p e j", e=2),
+                )
+                nc.sync.dma_start(
+                    out=dst[:, part, 2:4, HALF:T],
+                    in_=S_parts[part][b, HALF:T, HALF:T].rearrange("(p e) j -> p e j", e=2),
+                )
+
+        load_E(0)
+        load_S(0)
+        w_raw = const.tile([P, 2, C], BF16, name="w_raw")
+        for part in (RE, IM):
+            nc.sync.dma_start(out=w_raw[:, part, :], in_=W_parts[part])
+        for b in range(1, RAW_BUFS):
+            load_E(b)
+            load_S(b)
+
+        ident = const.tile([P, P], F32, name="ident")
+        make_identity(nc, ident[:])
+
+        mask_idx = const.tile([P, 2, HALF], I32, name="mask_idx")
+        nc.gpsimd.iota(mask_idx[:], pattern=[[-1, 2], [1, HALF]], base=0, channel_multiplier=-2)
+        mask = const.tile([P, 2, HALF], BF16, name="mask")
+        nc.vector.tensor_single_scalar(out=mask[:], in_=mask_idx[:], scalar=0.0, op=ALU.is_ge)
+
+        j_idx = const.tile([P, T], I32, name="j_idx")
+        nc.gpsimd.iota(j_idx[:], pattern=[[1, T]], base=0, channel_multiplier=0)
+        rho = const.tile([P, T], F32, name="rho")
+        nc.vector.tensor_scalar_max(out=rho[:], in0=j_idx[:], scalar1=1.0)
+        inv_rho = const.tile([P, T], F32, name="inv_rho")
+        nc.vector.reciprocal(out=inv_rho[:], in_=rho[:])
+
+        w_words = w_raw[:].bitcast(F32).rearrange("o a (m h) -> o a h m", h=2)
+        w_bank = psum.tile([P, 2, 2, O], F32, name="w_bank", tag="bank")
+        for part in (RE, IM):
+            for h in range(2):
+                nc.tensor.transpose(w_bank[:, part, h, :], w_words[:, part, h, :], ident[:])
+        p_grouped = const.tile([P, 3, O, PACK], BF16, name="p_grouped", align_bytes=64)
+        nc.vector.tensor_copy(
+            out=p_grouped[:].bitcast(F32)[:, RE : IM + 1],
+            in_=w_bank[:].rearrange("p a h o -> p a o h"),
+        )
+        nc.vector.tensor_scalar_mul(
+            out=p_grouped[:, NEG_IM], in0=p_grouped[:, IM], scalar1=-1.0
+        )
+        p_codes = const.tile([P, 3, O], U32, name="p_codes", align_bytes=64)
+        p_scales = const.tile([P, 3, O], U8, name="p_scales", align_bytes=64)
+        for slot in (RE, IM, NEG_IM):
+            nc.vector.quantize_mx(
+                out=p_codes[:, slot, :].bitcast(FP8X4),
+                scales=p_scales[:, slot, :],
+                in_=p_grouped[:, slot].rearrange("p o t -> p (o t)"),
+            )
+
+        e_codes, e_scales = {}, {}
+        m_codes, m_scales = {}, {}
+        v_grouped, v_codes, v_scales = {}, {}, {}
+
+        def prepare_E(b):
+            e_words = e_raw[b][:].bitcast(F32)
+            e_grouped = work.tile([P, 3, C, PACK], BF16, name="e_grouped", align_bytes=64)
+            e_grouped_words = e_grouped[:].bitcast(F32)
+            e_codes[b] = work.tile([P, 3, C], U32, name="e_codes", align_bytes=64)
+            e_scales[b] = work.tile([P, 3, C], U8, name="e_scales", align_bytes=64)
+            for part in (RE, IM):
+                for pair in range(2):
+                    e_bank = psum.tile([P, 2, 2, P], F32, name="e_bank", tag="bank")
+                    for a in range(2):
+                        for u in range(2):
+                            nc.tensor.transpose(
+                                e_bank[:, a, u, :],
+                                e_words[:, part, 2 * pair + a, P * u : P * (u + 1)],
+                                ident[:],
+                            )
+                    nc.scalar.copy(
+                        out=e_grouped_words[
+                            :, part, 2 * P * pair : 2 * P * (pair + 1), :
+                        ].rearrange("p (a m) u -> p a m u", a=2),
+                        in_=e_bank[:].rearrange("p a u m -> p a m u"),
+                    )
+            nc.vector.tensor_scalar_mul(
+                out=e_grouped[:, NEG_IM].rearrange("p c t -> p (c t)"),
+                in0=e_grouped[:, IM].rearrange("p c t -> p (c t)"),
+                scalar1=-1.0,
+            )
+            for slot in (RE, IM, NEG_IM):
+                nc.vector.quantize_mx(
+                    out=e_codes[b][:, slot, :].bitcast(FP8X4),
+                    scales=e_scales[b][:, slot, :],
+                    in_=e_grouped[:, slot].rearrange("p c t -> p (c t)"),
+                )
+
+        def prepare_M(b):
+            src = s_raw[b % RAW_BUFS]
+            for u in range(2):
+                square = src[:, :, 2 * u : 2 * u + 2, HALF * u : HALF * (u + 1)]
+                nc.vector.tensor_tensor(
+                    out=square,
+                    in0=square,
+                    in1=mask[:].unsqueeze(1).to_broadcast([P, 2, 2, HALF]),
+                    op=ALU.mult,
+                )
+            m_grouped = work.tile([P, 2, T, PACK], BF16, name="m_grouped", align_bytes=64)
+            m_codes[b] = work.tile([P, 2, T], U32, name="m_codes", align_bytes=64)
+            m_scales[b] = work.tile([P, 2, T], U8, name="m_scales", align_bytes=64)
+            split = J_VECTOR // 4
+            for part in (RE, IM):
+                rows = src[:, part].rearrange("p t (g i) -> p g t i", i=4)
+                cols = m_grouped[:, part].rearrange("p (g i) t -> p g t i", i=4)
+                nc.vector.tensor_copy(out=cols[:, :split], in_=rows[:, :split])
+                nc.scalar.copy(out=cols[:, split:], in_=rows[:, split:])
+            for part in (RE, IM):
+                nc.vector.quantize_mx(
+                    out=m_codes[b][:, part, :].bitcast(FP8X4),
+                    scales=m_scales[b][:, part, :],
+                    in_=m_grouped[:, part].rearrange("p j t -> p (j t)"),
+                )
+
+        def first_matmul(b, part):
+            if part == RE:
+                products = ((RE, RE), (NEG_IM, IM))
+                v_grouped[b] = work.tile([P, 2, T, PACK], BF16, name="v_grouped", align_bytes=64)
+                v_codes[b] = work.tile([P, 2, T], U32, name="v_codes", align_bytes=64)
+                v_scales[b] = work.tile([P, 2, T], U8, name="v_scales", align_bytes=64)
+            else:
+                products = ((RE, IM), (IM, RE))
+            for jt in range(T // P):
+                j_cols = slice(P * jt, P * (jt + 1))
+                v_bank = psum.tile([P, PACK, P], F32, name="v_bank", tag="bank")
+                for ct in range(PACK):
+                    c_cols = slice(P * ct, P * (ct + 1))
+                    for n, (e_slot, m_part) in enumerate(products):
+                        nc.tensor.matmul_mx(
+                            out=v_bank[:, ct, :],
+                            lhsT=e_codes[b][:, e_slot, c_cols].bitcast(FP8X4),
+                            lhsT_scale=e_scales[b][:, e_slot, c_cols],
+                            rhs=m_codes[b][:, m_part, j_cols].bitcast(FP8X4),
+                            rhs_scale=m_scales[b][:, m_part, j_cols],
+                            start=(n == 0),
+                            stop=(n == 1),
+                        )
+                nc.scalar.copy(
+                    out=v_grouped[b][:, part, j_cols, :],
+                    in_=v_bank[:].rearrange("p t j -> p j t"),
+                )
+            nc.vector.quantize_mx(
+                out=v_codes[b][:, part, :].bitcast(FP8X4),
+                scales=v_scales[b][:, part, :],
+                in_=v_grouped[b][:, part].rearrange("p j t -> p (j t)"),
+            )
+
+        def second_matmul(b):
+            result = out_pool.tile([P, 2, T], F32, name="result")
+            for part in (RE, IM):
+                if part == RE:
+                    products = ((RE, RE), (NEG_IM, IM))
+                else:
+                    products = ((RE, IM), (IM, RE))
+                o_bank = psum.tile([P, T], F32, name="o_bank", tag="bank")
+                for n, (p_slot, v_part) in enumerate(products):
+                    nc.tensor.matmul_mx(
+                        out=o_bank[:],
+                        lhsT=p_codes[:, p_slot, :].bitcast(FP8X4),
+                        lhsT_scale=p_scales[:, p_slot, :],
+                        rhs=v_codes[b][:, v_part, :].bitcast(FP8X4),
+                        rhs_scale=v_scales[b][:, v_part, :],
+                        start=(n == 0),
+                        stop=(n == 1),
+                    )
+                nc.vector.tensor_tensor(
+                    out=result[:, part, :], in0=o_bank[:], in1=inv_rho[:], op=ALU.mult
+                )
+                nc.sync.dma_start(out=out_parts[part][b], in_=result[:, part, :])
+
+        def prepare(b):
+            prepare_E(b)
+            prepare_M(b)
+            if b + RAW_BUFS < B:
+                load_E(b + RAW_BUFS)
+                load_S(b + RAW_BUFS)
+
+        prepare(0)
+        for b in range(B):
+            if b + 1 < B:
+                prepare(b + 1)
+            first_matmul(b, RE)
+            if b > 0:
+                second_matmul(b - 1)
+            first_matmul(b, IM)
+        second_matmul(B - 1)

@@ -21,9 +21,12 @@ HALF = T // 2
 RE = 0
 IM = 1
 NEG_IM = 2
+PRODUCTS = {
+    RE: ((RE, RE), (NEG_IM, IM)),
+    IM: ((IM, RE), (RE, IM)),
+}
 
 RAW_BUFS = 4
-J_VECTOR = 320
 
 FLOPS = 4 * 2 * B * C * T * T + 4 * 2 * B * O * C * T
 
@@ -37,49 +40,58 @@ def tile_autoregressivelsa_pb_t_kernel(
     W_parts = (WPV_re, WPV_im)
     out_parts = (out_re, out_im)
 
+    def quantise(values, codes, scales):
+        nc.vector.quantize_mx(
+            out=codes.bitcast(FP8X4),
+            scales=scales,
+            in_=values.rearrange("p w t -> p (w t)"),
+        )
+
+    def multiply(bank, left, right, cols_left, cols_right, first, last):
+        nc.tensor.matmul_mx(
+            out=bank,
+            lhsT=left[0][:, cols_left].bitcast(FP8X4),
+            lhsT_scale=left[1][:, cols_left],
+            rhs=right[0][:, cols_right].bitcast(FP8X4),
+            rhs_scale=right[1][:, cols_right],
+            start=first,
+            stop=last,
+        )
+
     with ExitStack() as ctx:
         const = ctx.enter_context(tc.tile_pool(name="const", bufs=1))
-        e_pool = ctx.enter_context(tc.tile_pool(name="e_raw", bufs=RAW_BUFS))
+        raw = ctx.enter_context(tc.tile_pool(name="raw", bufs=RAW_BUFS))
         work = ctx.enter_context(tc.tile_pool(name="work", bufs=2))
         out_pool = ctx.enter_context(tc.tile_pool(name="out", bufs=3))
         psum = ctx.enter_context(tc.psum_pool(name="psum", bufs=8))
 
-        e_raw = {}
+        e_raw, s_raw = {}, {}
 
-        def load_E(b):
-            e_raw[b] = e_pool.tile([P, 2, PACK, T], BF16, name="e_raw")
+        def load(b):
+            e_raw[b] = raw.tile([P, 2, PACK, T], BF16, name="e_raw")
             for part in (RE, IM):
                 nc.sync.dma_start(
                     out=e_raw[b][:, part],
                     in_=E_parts[part][b].rearrange("(p t) i -> p t i", t=PACK),
                 )
-
-        s_raw = [
-            const.tile([P, 2, PACK, T], BF16, name="s_raw%d" % k) for k in range(RAW_BUFS)
-        ]
-        for k in range(RAW_BUFS):
-            nc.vector.memset(s_raw[k][:, :, 2:4, 0:HALF], 0.0)
-
-        def load_S(b):
-            dst = s_raw[b % RAW_BUFS]
+            s_raw[b] = raw.tile([P, 2, PACK, T], BF16, name="s_raw")
             for part in (RE, IM):
                 nc.sync.dma_start(
-                    out=dst[:, part, 0:2, :],
+                    out=s_raw[b][:, part, 0:2, :],
                     in_=S_parts[part][b, 0:HALF, :].rearrange("(p e) j -> p e j", e=2),
                 )
                 nc.sync.dma_start(
-                    out=dst[:, part, 2:4, HALF:T],
+                    out=s_raw[b][:, part, 2:4, HALF:T],
                     in_=S_parts[part][b, HALF:T, HALF:T].rearrange("(p e) j -> p e j", e=2),
                 )
 
-        load_E(0)
-        load_S(0)
+        load(0)
+        load(1)
         w_raw = const.tile([P, 2, C], BF16, name="w_raw")
         for part in (RE, IM):
             nc.sync.dma_start(out=w_raw[:, part, :], in_=W_parts[part])
-        for b in range(1, RAW_BUFS):
-            load_E(b)
-            load_S(b)
+        for b in range(2, RAW_BUFS):
+            load(b)
 
         ident = const.tile([P, P], F32, name="ident")
         make_identity(nc, ident[:])
@@ -96,38 +108,41 @@ def tile_autoregressivelsa_pb_t_kernel(
         inv_rho = const.tile([P, T], F32, name="inv_rho")
         nc.vector.reciprocal(out=inv_rho[:], in_=rho[:])
 
-        w_words = w_raw[:].bitcast(F32).rearrange("o a (m h) -> o a h m", h=2)
-        w_bank = psum.tile([P, 2, 2, O], F32, name="w_bank", tag="bank")
-        for part in (RE, IM):
-            for h in range(2):
-                nc.tensor.transpose(w_bank[:, part, h, :], w_words[:, part, h, :], ident[:])
-        p_grouped = const.tile([P, 3, O, PACK], BF16, name="p_grouped", align_bytes=64)
-        nc.vector.tensor_copy(
-            out=p_grouped[:].bitcast(F32)[:, RE : IM + 1],
-            in_=w_bank[:].rearrange("p a h o -> p a o h"),
-        )
-        nc.vector.tensor_scalar_mul(
-            out=p_grouped[:, NEG_IM], in0=p_grouped[:, IM], scalar1=-1.0
-        )
+        m_grouped = [
+            const.tile([P, 2, T, PACK], BF16, name="m_grouped%d" % k, align_bytes=64)
+            for k in range(2)
+        ]
+        for k in range(2):
+            nc.vector.memset(m_grouped[k][:, :, 0:HALF, :], 0.0)
+
         p_codes = const.tile([P, 3, O], U32, name="p_codes", align_bytes=64)
         p_scales = const.tile([P, 3, O], U8, name="p_scales", align_bytes=64)
-        for slot in (RE, IM, NEG_IM):
-            nc.vector.quantize_mx(
-                out=p_codes[:, slot, :].bitcast(FP8X4),
-                scales=p_scales[:, slot, :],
-                in_=p_grouped[:, slot].rearrange("p o t -> p (o t)"),
+
+        def prepare_P():
+            w_words = w_raw[:].bitcast(F32).rearrange("o a (m h) -> o a h m", h=2)
+            w_bank = psum.tile([P, 2, 2, O], F32, name="w_bank", tag="bank")
+            for part in (RE, IM):
+                for h in range(2):
+                    nc.tensor.transpose(w_bank[:, part, h, :], w_words[:, part, h, :], ident[:])
+            p_grouped = const.tile([P, 3, O, PACK], BF16, name="p_grouped", align_bytes=64)
+            nc.vector.tensor_copy(
+                out=p_grouped[:].bitcast(F32)[:, RE : IM + 1],
+                in_=w_bank[:].rearrange("p a h o -> p a o h"),
             )
+            nc.vector.tensor_scalar_mul(
+                out=p_grouped[:, NEG_IM], in0=p_grouped[:, IM], scalar1=-1.0
+            )
+            for slot in (RE, IM, NEG_IM):
+                quantise(p_grouped[:, slot], p_codes[:, slot, :], p_scales[:, slot, :])
 
         e_codes, e_scales = {}, {}
         m_codes, m_scales = {}, {}
         v_grouped, v_codes, v_scales = {}, {}, {}
 
-        def prepare_E(b):
+        def prepare(b):
             e_words = e_raw[b][:].bitcast(F32)
             e_grouped = work.tile([P, 3, C, PACK], BF16, name="e_grouped", align_bytes=64)
             e_grouped_words = e_grouped[:].bitcast(F32)
-            e_codes[b] = work.tile([P, 3, C], U32, name="e_codes", align_bytes=64)
-            e_scales[b] = work.tile([P, 3, C], U8, name="e_scales", align_bytes=64)
             for part in (RE, IM):
                 for pair in range(2):
                     e_bank = psum.tile([P, 2, 2, P], F32, name="e_bank", tag="bank")
@@ -144,108 +159,101 @@ def tile_autoregressivelsa_pb_t_kernel(
                         ].rearrange("p (a m) u -> p a m u", a=2),
                         in_=e_bank[:].rearrange("p a u m -> p a m u"),
                     )
-            nc.vector.tensor_scalar_mul(
-                out=e_grouped[:, NEG_IM].rearrange("p c t -> p (c t)"),
-                in0=e_grouped[:, IM].rearrange("p c t -> p (c t)"),
-                scalar1=-1.0,
-            )
-            for slot in (RE, IM, NEG_IM):
-                nc.vector.quantize_mx(
-                    out=e_codes[b][:, slot, :].bitcast(FP8X4),
-                    scales=e_scales[b][:, slot, :],
-                    in_=e_grouped[:, slot].rearrange("p c t -> p (c t)"),
-                )
 
-        def prepare_M(b):
-            src = s_raw[b % RAW_BUFS]
             for u in range(2):
-                square = src[:, :, 2 * u : 2 * u + 2, HALF * u : HALF * (u + 1)]
+                square = s_raw[b][:, :, 2 * u : 2 * u + 2, HALF * u : HALF * (u + 1)]
                 nc.vector.tensor_tensor(
                     out=square,
                     in0=square,
                     in1=mask[:].unsqueeze(1).to_broadcast([P, 2, 2, HALF]),
                     op=ALU.mult,
                 )
-            m_grouped = work.tile([P, 2, T, PACK], BF16, name="m_grouped", align_bytes=64)
+            grouped = m_grouped[b % 2]
+            for part in (RE, IM):
+                nc.scalar.copy(
+                    out=grouped[:, part, 0:HALF, 0:2].rearrange("p (g i) t -> p g t i", i=4),
+                    in_=s_raw[b][:, part, 0:2, 0:HALF].rearrange("p t (g i) -> p g t i", i=4),
+                )
+                nc.vector.tensor_copy(
+                    out=grouped[:, part, HALF:T, :].rearrange("p (g i) t -> p g t i", i=4),
+                    in_=s_raw[b][:, part, :, HALF:T].rearrange("p t (g i) -> p g t i", i=4),
+                )
+
+            e_codes[b] = work.tile([P, 3, C], U32, name="e_codes", align_bytes=64)
+            e_scales[b] = work.tile([P, 3, C], U8, name="e_scales", align_bytes=64)
             m_codes[b] = work.tile([P, 2, T], U32, name="m_codes", align_bytes=64)
             m_scales[b] = work.tile([P, 2, T], U8, name="m_scales", align_bytes=64)
-            split = J_VECTOR // 4
-            for part in (RE, IM):
-                rows = src[:, part].rearrange("p t (g i) -> p g t i", i=4)
-                cols = m_grouped[:, part].rearrange("p (g i) t -> p g t i", i=4)
-                nc.vector.tensor_copy(out=cols[:, :split], in_=rows[:, :split])
-                nc.scalar.copy(out=cols[:, split:], in_=rows[:, split:])
-            for part in (RE, IM):
-                nc.vector.quantize_mx(
-                    out=m_codes[b][:, part, :].bitcast(FP8X4),
-                    scales=m_scales[b][:, part, :],
-                    in_=m_grouped[:, part].rearrange("p j t -> p (j t)"),
-                )
+
+            def quantise_E(slot):
+                quantise(e_grouped[:, slot], e_codes[b][:, slot, :], e_scales[b][:, slot, :])
+
+            def quantise_M(part):
+                quantise(grouped[:, part], m_codes[b][:, part, :], m_scales[b][:, part, :])
+
+            quantise_E(RE)
+            nc.vector.tensor_scalar_mul(
+                out=e_grouped[:, NEG_IM].rearrange("p c t -> p (c t)"),
+                in0=e_grouped[:, IM].rearrange("p c t -> p (c t)"),
+                scalar1=-1.0,
+            )
+            quantise_E(IM)
+            quantise_M(RE)
+            quantise_E(NEG_IM)
+            quantise_M(IM)
+
+            if b + RAW_BUFS < B:
+                load(b + RAW_BUFS)
 
         def first_matmul(b, part):
             if part == RE:
-                products = ((RE, RE), (NEG_IM, IM))
                 v_grouped[b] = work.tile([P, 2, T, PACK], BF16, name="v_grouped", align_bytes=64)
                 v_codes[b] = work.tile([P, 2, T], U32, name="v_codes", align_bytes=64)
                 v_scales[b] = work.tile([P, 2, T], U8, name="v_scales", align_bytes=64)
-            else:
-                products = ((RE, IM), (IM, RE))
             for jt in range(T // P):
                 j_cols = slice(P * jt, P * (jt + 1))
                 v_bank = psum.tile([P, PACK, P], F32, name="v_bank", tag="bank")
                 for ct in range(PACK):
-                    c_cols = slice(P * ct, P * (ct + 1))
-                    for n, (e_slot, m_part) in enumerate(products):
-                        nc.tensor.matmul_mx(
-                            out=v_bank[:, ct, :],
-                            lhsT=e_codes[b][:, e_slot, c_cols].bitcast(FP8X4),
-                            lhsT_scale=e_scales[b][:, e_slot, c_cols],
-                            rhs=m_codes[b][:, m_part, j_cols].bitcast(FP8X4),
-                            rhs_scale=m_scales[b][:, m_part, j_cols],
-                            start=(n == 0),
-                            stop=(n == 1),
+                    for n, (e_slot, m_part) in enumerate(PRODUCTS[part]):
+                        multiply(
+                            v_bank[:, ct, :],
+                            (e_codes[b][:, e_slot], e_scales[b][:, e_slot]),
+                            (m_codes[b][:, m_part], m_scales[b][:, m_part]),
+                            slice(P * ct, P * (ct + 1)),
+                            j_cols,
+                            n == 0,
+                            n == 1,
                         )
                 nc.scalar.copy(
                     out=v_grouped[b][:, part, j_cols, :],
                     in_=v_bank[:].rearrange("p t j -> p j t"),
                 )
-            nc.vector.quantize_mx(
-                out=v_codes[b][:, part, :].bitcast(FP8X4),
-                scales=v_scales[b][:, part, :],
-                in_=v_grouped[b][:, part].rearrange("p j t -> p (j t)"),
-            )
+            quantise(v_grouped[b][:, part], v_codes[b][:, part, :], v_scales[b][:, part, :])
 
         def second_matmul(b):
+            o_bank = {}
+            for part in (RE, IM):
+                o_bank[part] = psum.tile([P, T], F32, name="o_bank", tag="bank")
+            for n in range(2):
+                for part in (RE, IM):
+                    p_slot, v_part = PRODUCTS[part][n]
+                    multiply(
+                        o_bank[part][:],
+                        (p_codes[:, p_slot], p_scales[:, p_slot]),
+                        (v_codes[b][:, v_part], v_scales[b][:, v_part]),
+                        slice(0, O),
+                        slice(0, T),
+                        n == 0,
+                        n == 1,
+                    )
             result = out_pool.tile([P, 2, T], F32, name="result")
             for part in (RE, IM):
-                if part == RE:
-                    products = ((RE, RE), (NEG_IM, IM))
-                else:
-                    products = ((RE, IM), (IM, RE))
-                o_bank = psum.tile([P, T], F32, name="o_bank", tag="bank")
-                for n, (p_slot, v_part) in enumerate(products):
-                    nc.tensor.matmul_mx(
-                        out=o_bank[:],
-                        lhsT=p_codes[:, p_slot, :].bitcast(FP8X4),
-                        lhsT_scale=p_scales[:, p_slot, :],
-                        rhs=v_codes[b][:, v_part, :].bitcast(FP8X4),
-                        rhs_scale=v_scales[b][:, v_part, :],
-                        start=(n == 0),
-                        stop=(n == 1),
-                    )
                 nc.vector.tensor_tensor(
-                    out=result[:, part, :], in0=o_bank[:], in1=inv_rho[:], op=ALU.mult
+                    out=result[:, part, :], in0=o_bank[part][:], in1=inv_rho[:], op=ALU.mult
                 )
                 nc.sync.dma_start(out=out_parts[part][b], in_=result[:, part, :])
 
-        def prepare(b):
-            prepare_E(b)
-            prepare_M(b)
-            if b + RAW_BUFS < B:
-                load_E(b + RAW_BUFS)
-                load_S(b + RAW_BUFS)
-
         prepare(0)
+        prepare_P()
         for b in range(B):
             if b + 1 < B:
                 prepare(b + 1)

@@ -27,6 +27,7 @@ PRODUCTS = {
 }
 
 RAW_BUFS = 4
+J_SPLIT = 384
 
 FLOPS = 4 * 2 * B * C * T * T + 4 * 2 * B * O * C * T
 
@@ -68,12 +69,6 @@ def tile_autoregressivelsa_pb_t_kernel(
         e_raw, s_raw = {}, {}
 
         def load(b):
-            e_raw[b] = raw.tile([P, 2, PACK, T], BF16, name="e_raw")
-            for part in (RE, IM):
-                nc.sync.dma_start(
-                    out=e_raw[b][:, part],
-                    in_=E_parts[part][b].rearrange("(p t) i -> p t i", t=PACK),
-                )
             s_raw[b] = raw.tile([P, 2, PACK, T], BF16, name="s_raw")
             for part in (RE, IM):
                 nc.sync.dma_start(
@@ -84,13 +79,17 @@ def tile_autoregressivelsa_pb_t_kernel(
                     out=s_raw[b][:, part, 2:4, HALF:T],
                     in_=S_parts[part][b, HALF:T, HALF:T].rearrange("(p e) j -> p e j", e=2),
                 )
+            e_raw[b] = raw.tile([P, 2, PACK, T], BF16, name="e_raw")
+            for part in (RE, IM):
+                nc.sync.dma_start(
+                    out=e_raw[b][:, part],
+                    in_=E_parts[part][b].rearrange("(p t) i -> p t i", t=PACK),
+                )
 
-        load(0)
-        load(1)
         w_raw = const.tile([P, 2, C], BF16, name="w_raw")
         for part in (RE, IM):
             nc.sync.dma_start(out=w_raw[:, part, :], in_=W_parts[part])
-        for b in range(2, RAW_BUFS):
+        for b in range(RAW_BUFS):
             load(b)
 
         ident = const.tile([P, P], F32, name="ident")
@@ -137,12 +136,13 @@ def tile_autoregressivelsa_pb_t_kernel(
 
         e_codes, e_scales = {}, {}
         m_codes, m_scales = {}, {}
+        e_grouped = {}
         v_grouped, v_codes, v_scales = {}, {}, {}
 
-        def prepare(b):
+        def transpose_E(b):
             e_words = e_raw[b][:].bitcast(F32)
-            e_grouped = work.tile([P, 3, C, PACK], BF16, name="e_grouped", align_bytes=64)
-            e_grouped_words = e_grouped[:].bitcast(F32)
+            e_grouped[b] = work.tile([P, 3, C, PACK], BF16, name="e_grouped", align_bytes=64)
+            e_grouped_words = e_grouped[b][:].bitcast(F32)
             for part in (RE, IM):
                 for pair in range(2):
                     e_bank = psum.tile([P, 2, 2, P], F32, name="e_bank", tag="bank")
@@ -160,6 +160,7 @@ def tile_autoregressivelsa_pb_t_kernel(
                         in_=e_bank[:].rearrange("p a u m -> p a m u"),
                     )
 
+        def mask_and_regroup_S(b):
             for u in range(2):
                 square = s_raw[b][:, :, 2 * u : 2 * u + 2, HALF * u : HALF * (u + 1)]
                 nc.vector.tensor_tensor(
@@ -170,39 +171,44 @@ def tile_autoregressivelsa_pb_t_kernel(
                 )
             grouped = m_grouped[b % 2]
             for part in (RE, IM):
+                nc.vector.tensor_copy(
+                    out=grouped[:, part, HALF:J_SPLIT, :].rearrange("p (g i) t -> p g t i", i=4),
+                    in_=s_raw[b][:, part, :, HALF:J_SPLIT].rearrange("p t (g i) -> p g t i", i=4),
+                )
                 nc.scalar.copy(
                     out=grouped[:, part, 0:HALF, 0:2].rearrange("p (g i) t -> p g t i", i=4),
                     in_=s_raw[b][:, part, 0:2, 0:HALF].rearrange("p t (g i) -> p g t i", i=4),
                 )
-                nc.vector.tensor_copy(
-                    out=grouped[:, part, HALF:T, :].rearrange("p (g i) t -> p g t i", i=4),
-                    in_=s_raw[b][:, part, :, HALF:T].rearrange("p t (g i) -> p g t i", i=4),
+                nc.scalar.copy(
+                    out=grouped[:, part, J_SPLIT:T, :].rearrange("p (g i) t -> p g t i", i=4),
+                    in_=s_raw[b][:, part, :, J_SPLIT:T].rearrange("p t (g i) -> p g t i", i=4),
                 )
+            if b + RAW_BUFS < B:
+                load(b + RAW_BUFS)
 
+        def quantise_E_and_M(b):
+            grouped = m_grouped[b % 2]
             e_codes[b] = work.tile([P, 3, C], U32, name="e_codes", align_bytes=64)
             e_scales[b] = work.tile([P, 3, C], U8, name="e_scales", align_bytes=64)
             m_codes[b] = work.tile([P, 2, T], U32, name="m_codes", align_bytes=64)
             m_scales[b] = work.tile([P, 2, T], U8, name="m_scales", align_bytes=64)
 
             def quantise_E(slot):
-                quantise(e_grouped[:, slot], e_codes[b][:, slot, :], e_scales[b][:, slot, :])
+                quantise(e_grouped[b][:, slot], e_codes[b][:, slot, :], e_scales[b][:, slot, :])
 
             def quantise_M(part):
                 quantise(grouped[:, part], m_codes[b][:, part, :], m_scales[b][:, part, :])
 
             quantise_E(RE)
             nc.vector.tensor_scalar_mul(
-                out=e_grouped[:, NEG_IM].rearrange("p c t -> p (c t)"),
-                in0=e_grouped[:, IM].rearrange("p c t -> p (c t)"),
+                out=e_grouped[b][:, NEG_IM].rearrange("p c t -> p (c t)"),
+                in0=e_grouped[b][:, IM].rearrange("p c t -> p (c t)"),
                 scalar1=-1.0,
             )
             quantise_E(IM)
             quantise_M(RE)
             quantise_E(NEG_IM)
             quantise_M(IM)
-
-            if b + RAW_BUFS < B:
-                load(b + RAW_BUFS)
 
         def first_matmul(b, part):
             if part == RE:
@@ -227,6 +233,8 @@ def tile_autoregressivelsa_pb_t_kernel(
                     out=v_grouped[b][:, part, j_cols, :],
                     in_=v_bank[:].rearrange("p t j -> p j t"),
                 )
+
+        def quantise_V(b, part):
             quantise(v_grouped[b][:, part], v_codes[b][:, part, :], v_scales[b][:, part, :])
 
         def second_matmul(b):
@@ -252,13 +260,22 @@ def tile_autoregressivelsa_pb_t_kernel(
                 )
                 nc.sync.dma_start(out=out_parts[part][b], in_=result[:, part, :])
 
-        prepare(0)
         prepare_P()
+        transpose_E(0)
+        mask_and_regroup_S(0)
+        quantise_E_and_M(0)
         for b in range(B):
             if b + 1 < B:
-                prepare(b + 1)
+                transpose_E(b + 1)
+                mask_and_regroup_S(b + 1)
+            if b > 0:
+                quantise_V(b - 1, IM)
+            if b + 1 < B:
+                quantise_E_and_M(b + 1)
             first_matmul(b, RE)
             if b > 0:
                 second_matmul(b - 1)
+            quantise_V(b, RE)
             first_matmul(b, IM)
+        quantise_V(B - 1, IM)
         second_matmul(B - 1)

@@ -27,7 +27,6 @@ PRODUCTS = {
 }
 
 RAW_BUFS = 4
-J_SPLIT = 384
 
 FLOPS = 4 * 2 * B * C * T * T + 4 * 2 * B * O * C * T
 
@@ -75,6 +74,7 @@ def tile_autoregressivelsa_pb_t_kernel(
                     out=s_raw[b][:, part, 0:2, :],
                     in_=S_parts[part][b, 0:HALF, :].rearrange("(p e) j -> p e j", e=2),
                 )
+            for part in (RE, IM):
                 nc.sync.dma_start(
                     out=s_raw[b][:, part, 2:4, HALF:T],
                     in_=S_parts[part][b, HALF:T, HALF:T].rearrange("(p e) j -> p e j", e=2),
@@ -100,19 +100,32 @@ def tile_autoregressivelsa_pb_t_kernel(
         mask = const.tile([P, 2, HALF], BF16, name="mask")
         nc.vector.tensor_single_scalar(out=mask[:], in_=mask_idx[:], scalar=0.0, op=ALU.is_ge)
 
-        j_idx = const.tile([P, T], I32, name="j_idx")
-        nc.gpsimd.iota(j_idx[:], pattern=[[1, T]], base=0, channel_multiplier=0)
-        rho = const.tile([P, T], F32, name="rho")
-        nc.vector.tensor_scalar_max(out=rho[:], in0=j_idx[:], scalar1=1.0)
         inv_rho = const.tile([P, T], F32, name="inv_rho")
-        nc.vector.reciprocal(out=inv_rho[:], in_=rho[:])
+
+        def prepare_inv_rho():
+            j_idx = const.tile([P, T // P], I32, name="j_idx")
+            nc.gpsimd.iota(j_idx[:], pattern=[[P, T // P]], base=0, channel_multiplier=1)
+            rho_col = const.tile([P, T // P], F32, name="rho_col")
+            nc.vector.tensor_scalar_max(out=rho_col[:], in0=j_idx[:], scalar1=1.0)
+            inv_col = const.tile([P, T // P], F32, name="inv_col")
+            nc.vector.reciprocal(out=inv_col[:], in_=rho_col[:])
+            rho_bank = psum.tile([P, T], F32, name="rho_bank", tag="bank")
+            for m in range(T // P):
+                nc.tensor.matmul(
+                    out=rho_bank[:, P * m : P * (m + 1)],
+                    lhsT=inv_col[:, m : m + 1].to_broadcast([P, P]),
+                    rhs=ident[:],
+                    start=True,
+                    stop=True,
+                )
+            nc.scalar.copy(out=inv_rho[:], in_=rho_bank[:])
 
         m_grouped = [
             const.tile([P, 2, T, PACK], BF16, name="m_grouped%d" % k, align_bytes=64)
             for k in range(2)
         ]
         for k in range(2):
-            nc.vector.memset(m_grouped[k][:, :, 0:HALF, :], 0.0)
+            nc.vector.memset(m_grouped[k][:, :, 0:HALF, :].bitcast(I32), 0)
 
         p_codes = const.tile([P, 3, O], U32, name="p_codes", align_bytes=64)
         p_scales = const.tile([P, 3, O], U8, name="p_scales", align_bytes=64)
@@ -172,16 +185,12 @@ def tile_autoregressivelsa_pb_t_kernel(
             grouped = m_grouped[b % 2]
             for part in (RE, IM):
                 nc.vector.tensor_copy(
-                    out=grouped[:, part, HALF:J_SPLIT, :].rearrange("p (g i) t -> p g t i", i=4),
-                    in_=s_raw[b][:, part, :, HALF:J_SPLIT].rearrange("p t (g i) -> p g t i", i=4),
+                    out=grouped[:, part, HALF:T, :].rearrange("p (g i) t -> p g t i", i=4),
+                    in_=s_raw[b][:, part, :, HALF:T].rearrange("p t (g i) -> p g t i", i=4),
                 )
                 nc.scalar.copy(
                     out=grouped[:, part, 0:HALF, 0:2].rearrange("p (g i) t -> p g t i", i=4),
                     in_=s_raw[b][:, part, 0:2, 0:HALF].rearrange("p t (g i) -> p g t i", i=4),
-                )
-                nc.scalar.copy(
-                    out=grouped[:, part, J_SPLIT:T, :].rearrange("p (g i) t -> p g t i", i=4),
-                    in_=s_raw[b][:, part, :, J_SPLIT:T].rearrange("p t (g i) -> p g t i", i=4),
                 )
             if b + RAW_BUFS < B:
                 load(b + RAW_BUFS)
@@ -264,6 +273,7 @@ def tile_autoregressivelsa_pb_t_kernel(
         transpose_E(0)
         mask_and_regroup_S(0)
         quantise_E_and_M(0)
+        prepare_inv_rho()
         for b in range(B):
             if b + 1 < B:
                 transpose_E(b + 1)

@@ -26,6 +26,7 @@ PRODUCTS = {
     IM: ((IM, RE), (RE, IM)),
 }
 
+HOP = 8
 RAW_BUFS = 4
 
 FLOPS = 4 * 2 * B * C * T * T + 4 * 2 * B * O * C * T
@@ -185,12 +186,12 @@ def tile_autoregressivelsa_pb_t_kernel(
             grouped = m_grouped[b % 2]
             for part in (RE, IM):
                 nc.vector.tensor_copy(
-                    out=grouped[:, part, HALF:T, :].rearrange("p (g i) t -> p g t i", i=4),
-                    in_=s_raw[b][:, part, :, HALF:T].rearrange("p t (g i) -> p g t i", i=4),
+                    out=grouped[:, part, HALF:T, :].rearrange("p (g i) t -> p g t i", i=HOP),
+                    in_=s_raw[b][:, part, :, HALF:T].rearrange("p t (g i) -> p g t i", i=HOP),
                 )
                 nc.scalar.copy(
-                    out=grouped[:, part, 0:HALF, 0:2].rearrange("p (g i) t -> p g t i", i=4),
-                    in_=s_raw[b][:, part, 0:2, 0:HALF].rearrange("p t (g i) -> p g t i", i=4),
+                    out=grouped[:, part, 0:HALF, 0:2].rearrange("p (g i) t -> p g t i", i=HOP),
+                    in_=s_raw[b][:, part, 0:2, 0:HALF].rearrange("p t (g i) -> p g t i", i=HOP),
                 )
             if b + RAW_BUFS < B:
                 load(b + RAW_BUFS)

@@ -26,7 +26,7 @@ PRODUCTS = {
     IM: ((IM, RE), (RE, IM)),
 }
 
-HOP = 8
+HOP = 2
 RAW_BUFS = 4
 
 FLOPS = 4 * 2 * B * C * T * T + 4 * 2 * B * O * C * T

from contextlib import ExitStack

import concourse.mybir as mybir
from concourse.masks import make_identity

F32 = mybir.dt.float32
BF16 = mybir.dt.bfloat16
I32 = mybir.dt.int32
U32 = mybir.dt.uint32
U8 = mybir.dt.uint8
FP8X4 = mybir.dt.float8_e4m3fn_x4
ALU = mybir.AluOpType

B = 8
O = 128
C = 512
T = 512
P = 128
PACK = 4
HALF = T // 2
RE = 0
IM = 1
NEG_IM = 2
PRODUCTS = {
    RE: ((RE, RE), (NEG_IM, IM)),
    IM: ((IM, RE), (RE, IM)),
}

HOP = 2
RAW_BUFS = 4

FLOPS = 4 * 2 * B * C * T * T + 4 * 2 * B * O * C * T


def tile_autoregressivelsa_pb_t_kernel(
    tc, E_re, E_im, S_re, S_im, WPV_re, WPV_im, out_re, out_im
):
    nc = tc.nc
    E_parts = (E_re, E_im)
    S_parts = (S_re, S_im)
    W_parts = (WPV_re, WPV_im)
    out_parts = (out_re, out_im)

    def quantise(values, codes, scales):
        nc.vector.quantize_mx(
            out=codes.bitcast(FP8X4),
            scales=scales,
            in_=values.rearrange("p w t -> p (w t)"),
        )

    def multiply(bank, left, right, cols_left, cols_right, first, last):
        nc.tensor.matmul_mx(
            out=bank,
            lhsT=left[0][:, cols_left].bitcast(FP8X4),
            lhsT_scale=left[1][:, cols_left],
            rhs=right[0][:, cols_right].bitcast(FP8X4),
            rhs_scale=right[1][:, cols_right],
            start=first,
            stop=last,
        )

    with ExitStack() as ctx:
        const = ctx.enter_context(tc.tile_pool(name="const", bufs=1))
        raw = ctx.enter_context(tc.tile_pool(name="raw", bufs=RAW_BUFS))
        work = ctx.enter_context(tc.tile_pool(name="work", bufs=2))
        out_pool = ctx.enter_context(tc.tile_pool(name="out", bufs=3))
        psum = ctx.enter_context(tc.psum_pool(name="psum", bufs=8))

        e_raw, s_raw = {}, {}

        def load(b):
            s_raw[b] = raw.tile([P, 2, PACK, T], BF16, name="s_raw")
            for part in (RE, IM):
                nc.sync.dma_start(
                    out=s_raw[b][:, part, 0:2, :],
                    in_=S_parts[part][b, 0:HALF, :].rearrange("(p e) j -> p e j", e=2),
                )
            for part in (RE, IM):
                nc.sync.dma_start(
                    out=s_raw[b][:, part, 2:4, HALF:T],
                    in_=S_parts[part][b, HALF:T, HALF:T].rearrange("(p e) j -> p e j", e=2),
                )
            e_raw[b] = raw.tile([P, 2, PACK, T], BF16, name="e_raw")
            for part in (RE, IM):
                nc.sync.dma_start(
                    out=e_raw[b][:, part],
                    in_=E_parts[part][b].rearrange("(p t) i -> p t i", t=PACK),
                )

        w_raw = const.tile([P, 2, C], BF16, name="w_raw")
        for part in (RE, IM):
            nc.sync.dma_start(out=w_raw[:, part, :], in_=W_parts[part])
        for b in range(RAW_BUFS):
            load(b)

        ident = const.tile([P, P], F32, name="ident")
        make_identity(nc, ident[:])

        mask_idx = const.tile([P, 2, HALF], I32, name="mask_idx")
        nc.gpsimd.iota(mask_idx[:], pattern=[[-1, 2], [1, HALF]], base=0, channel_multiplier=-2)
        mask = const.tile([P, 2, HALF], BF16, name="mask")
        nc.vector.tensor_single_scalar(out=mask[:], in_=mask_idx[:], scalar=0.0, op=ALU.is_ge)

        inv_rho = const.tile([P, T], F32, name="inv_rho")

        def prepare_inv_rho():
            j_idx = const.tile([P, T // P], I32, name="j_idx")
            nc.gpsimd.iota(j_idx[:], pattern=[[P, T // P]], base=0, channel_multiplier=1)
            rho_col = const.tile([P, T // P], F32, name="rho_col")
            nc.vector.tensor_scalar_max(out=rho_col[:], in0=j_idx[:], scalar1=1.0)
            inv_col = const.tile([P, T // P], F32, name="inv_col")
            nc.vector.reciprocal(out=inv_col[:], in_=rho_col[:])
            rho_bank = psum.tile([P, T], F32, name="rho_bank", tag="bank")
            for m in range(T // P):
                nc.tensor.matmul(
                    out=rho_bank[:, P * m : P * (m + 1)],
                    lhsT=inv_col[:, m : m + 1].to_broadcast([P, P]),
                    rhs=ident[:],
                    start=True,
                    stop=True,
                )
            nc.scalar.copy(out=inv_rho[:], in_=rho_bank[:])

        m_grouped = [
            const.tile([P, 2, T, PACK], BF16, name="m_grouped%d" % k, align_bytes=64)
            for k in range(2)
        ]
        for k in range(2):
            nc.vector.memset(m_grouped[k][:, :, 0:HALF, :].bitcast(I32), 0)

        p_codes = const.tile([P, 3, O], U32, name="p_codes", align_bytes=64)
        p_scales = const.tile([P, 3, O], U8, name="p_scales", align_bytes=64)

        def prepare_P():
            w_words = w_raw[:].bitcast(F32).rearrange("o a (m h) -> o a h m", h=2)
            w_bank = psum.tile([P, 2, 2, O], F32, name="w_bank", tag="bank")
            for part in (RE, IM):
                for h in range(2):
                    nc.tensor.transpose(w_bank[:, part, h, :], w_words[:, part, h, :], ident[:])
            p_grouped = const.tile([P, 3, O, PACK], BF16, name="p_grouped", align_bytes=64)
            nc.vector.tensor_copy(
                out=p_grouped[:].bitcast(F32)[:, RE : IM + 1],
                in_=w_bank[:].rearrange("p a h o -> p a o h"),
            )
            nc.vector.tensor_scalar_mul(
                out=p_grouped[:, NEG_IM], in0=p_grouped[:, IM], scalar1=-1.0
            )
            for slot in (RE, IM, NEG_IM):
                quantise(p_grouped[:, slot], p_codes[:, slot, :], p_scales[:, slot, :])

        e_codes, e_scales = {}, {}
        m_codes, m_scales = {}, {}
        e_grouped = {}
        v_grouped, v_codes, v_scales = {}, {}, {}

        def transpose_E(b):
            e_words = e_raw[b][:].bitcast(F32)
            e_grouped[b] = work.tile([P, 3, C, PACK], BF16, name="e_grouped", align_bytes=64)
            e_grouped_words = e_grouped[b][:].bitcast(F32)
            for part in (RE, IM):
                for pair in range(2):
                    e_bank = psum.tile([P, 2, 2, P], F32, name="e_bank", tag="bank")
                    for a in range(2):
                        for u in range(2):
                            nc.tensor.transpose(
                                e_bank[:, a, u, :],
                                e_words[:, part, 2 * pair + a, P * u : P * (u + 1)],
                                ident[:],
                            )
                    nc.scalar.copy(
                        out=e_grouped_words[
                            :, part, 2 * P * pair : 2 * P * (pair + 1), :
                        ].rearrange("p (a m) u -> p a m u", a=2),
                        in_=e_bank[:].rearrange("p a u m -> p a m u"),
                    )

        def mask_and_regroup_S(b):
            for u in range(2):
                square = s_raw[b][:, :, 2 * u : 2 * u + 2, HALF * u : HALF * (u + 1)]
                nc.vector.tensor_tensor(
                    out=square,
                    in0=square,
                    in1=mask[:].unsqueeze(1).to_broadcast([P, 2, 2, HALF]),
                    op=ALU.mult,
                )
            grouped = m_grouped[b % 2]
            for part in (RE, IM):
                nc.vector.tensor_copy(
                    out=grouped[:, part, HALF:T, :].rearrange("p (g i) t -> p g t i", i=HOP),
                    in_=s_raw[b][:, part, :, HALF:T].rearrange("p t (g i) -> p g t i", i=HOP),
                )
                nc.scalar.copy(
                    out=grouped[:, part, 0:HALF, 0:2].rearrange("p (g i) t -> p g t i", i=HOP),
                    in_=s_raw[b][:, part, 0:2, 0:HALF].rearrange("p t (g i) -> p g t i", i=HOP),
                )
            if b + RAW_BUFS < B:
                load(b + RAW_BUFS)

        def quantise_E_and_M(b):
            grouped = m_grouped[b % 2]
            e_codes[b] = work.tile([P, 3, C], U32, name="e_codes", align_bytes=64)
            e_scales[b] = work.tile([P, 3, C], U8, name="e_scales", align_bytes=64)
            m_codes[b] = work.tile([P, 2, T], U32, name="m_codes", align_bytes=64)
            m_scales[b] = work.tile([P, 2, T], U8, name="m_scales", align_bytes=64)

            def quantise_E(slot):
                quantise(e_grouped[b][:, slot], e_codes[b][:, slot, :], e_scales[b][:, slot, :])

            def quantise_M(part):
                quantise(grouped[:, part], m_codes[b][:, part, :], m_scales[b][:, part, :])

            quantise_E(RE)
            nc.vector.tensor_scalar_mul(
                out=e_grouped[b][:, NEG_IM].rearrange("p c t -> p (c t)"),
                in0=e_grouped[b][:, IM].rearrange("p c t -> p (c t)"),
                scalar1=-1.0,
            )
            quantise_E(IM)
            quantise_M(RE)
            quantise_E(NEG_IM)
            quantise_M(IM)

        def first_matmul(b, part):
            if part == RE:
                v_grouped[b] = work.tile([P, 2, T, PACK], BF16, name="v_grouped", align_bytes=64)
                v_codes[b] = work.tile([P, 2, T], U32, name="v_codes", align_bytes=64)
                v_scales[b] = work.tile([P, 2, T], U8, name="v_scales", align_bytes=64)
            for jt in range(T // P):
                j_cols = slice(P * jt, P * (jt + 1))
                v_bank = psum.tile([P, PACK, P], F32, name="v_bank", tag="bank")
                for ct in range(PACK):
                    for n, (e_slot, m_part) in enumerate(PRODUCTS[part]):
                        multiply(
                            v_bank[:, ct, :],
                            (e_codes[b][:, e_slot], e_scales[b][:, e_slot]),
                            (m_codes[b][:, m_part], m_scales[b][:, m_part]),
                            slice(P * ct, P * (ct + 1)),
                            j_cols,
                            n == 0,
                            n == 1,
                        )
                nc.scalar.copy(
                    out=v_grouped[b][:, part, j_cols, :],
                    in_=v_bank[:].rearrange("p t j -> p j t"),
                )

        def quantise_V(b, part):
            quantise(v_grouped[b][:, part], v_codes[b][:, part, :], v_scales[b][:, part, :])

        def second_matmul(b):
            o_bank = {}
            for part in (RE, IM):
                o_bank[part] = psum.tile([P, T], F32, name="o_bank", tag="bank")
            for n in range(2):
                for part in (RE, IM):
                    p_slot, v_part = PRODUCTS[part][n]
                    multiply(
                        o_bank[part][:],
                        (p_codes[:, p_slot], p_scales[:, p_slot]),
                        (v_codes[b][:, v_part], v_scales[b][:, v_part]),
                        slice(0, O),
                        slice(0, T),
                        n == 0,
                        n == 1,
                    )
            result = out_pool.tile([P, 2, T], F32, name="result")
            for part in (RE, IM):
                nc.vector.tensor_tensor(
                    out=result[:, part, :], in0=o_bank[part][:], in1=inv_rho[:], op=ALU.mult
                )
                nc.sync.dma_start(out=out_parts[part][b], in_=result[:, part, :])

        prepare_P()
        transpose_E(0)
        mask_and_regroup_S(0)
        quantise_E_and_M(0)
        prepare_inv_rho()
        for b in range(B):
            if b + 1 < B:
                transpose_E(b + 1)
                mask_and_regroup_S(b + 1)
            if b > 0:
                quantise_V(b - 1, IM)
            if b + 1 < B:
                quantise_E_and_M(b + 1)
            first_matmul(b, RE)
            if b > 0:
                second_matmul(b - 1)
            quantise_V(b, RE)
            first_matmul(b, IM)
        quantise_V(B - 1, IM)
        second_matmul(B - 1)
